import numpy as np
import ml_dtypes


def mxq(x, axis, fmt="e4m3"):
    dtype, down = {"e4m3": (ml_dtypes.float8_e4m3fn, 7), "e5m2": (ml_dtypes.float8_e5m2, 14)}[fmt]
    v = np.moveaxis(np.asarray(x, np.float32).astype(ml_dtypes.bfloat16).astype(np.float64), axis, -1)
    blocks = v.reshape(v.shape[:-1] + (-1, 32))
    amax = np.abs(blocks).max(-1, keepdims=True)
    byte = np.maximum(np.where(amax > 0, np.frexp(amax)[1] - 1 + 127, 0) - down, 1)
    scale = np.exp2(byte - 127.0)
    codes = (blocks / scale).astype(np.float32).astype(dtype).astype(np.float64)
    return np.moveaxis((codes * scale).reshape(v.shape), -1, axis)


WIDE = False


def mx_kscale(k):
    if not WIDE:
        return np.ones(k)
    levels = np.array([10, -10, 5, -5, 0])
    a = np.random.permutation(np.resize(levels, k // 512 * 4)).reshape(k // 512, 4)
    idx = np.arange(k)
    return np.exp2(a[idx // 512, idx % 128 // 32])


BF16 = ml_dtypes.bfloat16


def bf(x):
    return np.asarray(x, np.float32).astype(BF16)


def f64(x):
    return np.asarray(x).astype(np.float64)


N, S, D, H, O = 4, 256, 1024, 1024, 1024


def elu(v):
    return np.where(v > 0.0, v, np.exp(np.minimum(v, 0.0)) - 1.0)


def setup_inputs():
    s = mx_kscale(D)
    return {"x": bf(np.random.standard_normal((N, S, D)) * s),
            "Wk": bf(np.random.standard_normal((D, H)) / np.sqrt(D) / s[:, None]),
            "bk": bf(np.random.standard_normal(H) * 0.1),
            "Wv": bf(np.random.standard_normal((D, H)) / np.sqrt(D) / s[:, None]),
            "bv": bf(np.random.standard_normal(H) * 0.1)}


def reference(x, Wk, bk, Wv, bv):
    xq = mxq(f64(x), 2, "e4m3")
    keyp = (xq @ mxq(f64(Wk), 0, "e4m3")) + f64(bk)
    value = (xq @ mxq(f64(Wv), 0, "e4m3")) + f64(bv)
    K = elu(keyp) + 1.0
    KV = np.sum(K * value, axis=1)
    Ksum = np.sum(K, axis=1)
    return KV, Ksum

@@ -1,0 +1,232 @@
+from contextlib import ExitStack
+from itertools import product
+
+import concourse.mybir as mybir
+from concourse.masks import make_identity
+
+F32 = mybir.dt.float32
+BF16 = mybir.dt.bfloat16
+U32 = mybir.dt.uint32
+U8 = mybir.dt.uint8
+FP8X4 = mybir.dt.float8_e4m3fn_x4
+ALU = mybir.AluOpType
+ACT = mybir.ActivationFunctionType
+
+BATCHES, SEQ, D, H = 4, 256, 1024, 1024
+TOKENS = BATCHES * SEQ
+
+P = 128
+PACK = 4
+K_PASS = P * PACK
+PASSES = D // K_PASS
+WORDS = PACK // 2
+
+N_MOVE = 512
+HALVES = TOKENS // N_MOVE
+TILES_PER_HALF = N_MOVE // P
+BATCHES_PER_HALF = N_MOVE // SEQ
+
+H_TILES = H // P
+CHUNK = 256
+CHUNKS = H // CHUNK
+TILES_PER_CHUNK = CHUNK // P
+WEIGHTS = 2
+PIECES = WEIGHTS * PASSES * CHUNKS
+
+RUN = 4
+VECTOR_COLS = 128
+
+FLOPS = 2 * WEIGHTS * TOKENS * D * H
+
+
+def tile_linearattention_pa_kernel(tc, x, Wk, bk, Wv, bv, out_0, out_1):
+    nc = tc.nc
+    x_rows = x.rearrange("n s d -> (n s) d")
+    weights = (Wk, Wv)
+
+    with ExitStack() as ctx:
+        consts = ctx.enter_context(tc.tile_pool(name="consts", bufs=1))
+        x_pool = ctx.enter_context(tc.tile_pool(name="x_pool", bufs=1))
+        w_pool = ctx.enter_context(tc.tile_pool(name="w_pool", bufs=PIECES))
+        group_pool = ctx.enter_context(tc.tile_pool(name="group_pool", bufs=4))
+        work = ctx.enter_context(tc.tile_pool(name="work", bufs=3))
+        psum = ctx.enter_context(tc.psum_pool(name="psum", bufs=2))
+
+        x_raw = {}
+        w_raw = {}
+
+        def load_x_half(half):
+            for a in range(TILES_PER_HALF):
+                tokens = slice((half * TILES_PER_HALF + a) * P, (half * TILES_PER_HALF + a + 1) * P)
+                raw = x_pool.tile([P, D], BF16, tag="x_raw", bufs=HALVES * TILES_PER_HALF)
+                nc.sync.dma_start(out=raw[:], in_=x_rows[tokens, :])
+                x_raw[(half, a)] = raw
+
+        def load_weight_chunk(c):
+            for w, g in product(range(WEIGHTS), range(PASSES)):
+                raw = w_pool.tile([P, PACK, CHUNK], BF16, tag="w_raw")
+                nc.sync.dma_start(
+                    out=raw[:],
+                    in_=weights[w][g * K_PASS : (g + 1) * K_PASS, c * CHUNK : (c + 1) * CHUNK].rearrange(
+                        "(p j) c -> p j c", j=PACK
+                    ),
+                )
+                w_raw[(w, g, c)] = raw
+
+        load_x_half(0)
+        load_weight_chunk(0)
+        load_x_half(1)
+        for c in range(1, CHUNKS):
+            load_weight_chunk(c)
+
+        ident = consts.tile([P, P], F32)
+        make_identity(nc, ident[:])
+
+        warm = consts.tile([P, 1], F32)
+        nc.vector.memset(warm[:], 0.0)
+        nc.scalar.activation(out=warm[:], in_=warm[:], func=ACT.Exp)
+
+        bias_rows = consts.tile([P, P], BF16)
+        nc.vector.memset(bias_rows[:], 0.0)
+        nc.scalar.dma_start(out=bias_rows[0:H_TILES, :], in_=bk.rearrange("(t p) -> t p", p=P))
+        nc.scalar.dma_start(out=bias_rows[H_TILES : 2 * H_TILES, :], in_=bv.rearrange("(t p) -> t p", p=P))
+        bias_rows_f32 = consts.tile([P, P], F32)
+        nc.vector.tensor_copy(out=bias_rows_f32[:], in_=bias_rows[:])
+        bias_ps = psum.tile([P, P], F32, tag="transposed")
+        nc.tensor.transpose(out=bias_ps[:], in_=bias_rows_f32[:], identity=ident[:])
+        bias_cols = consts.tile([P, 2 * H_TILES], F32)
+        nc.vector.tensor_copy(out=bias_cols[:], in_=bias_ps[:, 0 : 2 * H_TILES])
+        bk_plus_1 = consts.tile([P, H_TILES], F32)
+        nc.vector.tensor_scalar_add(out=bk_plus_1[:], in0=bias_ps[:, 0:H_TILES], scalar1=1.0)
+
+        sums = consts.tile([P, P], F32)
+        nc.vector.memset(sums[:], 0.0)
+
+        x_quant = {}
+
+        def prepare_x_half(half):
+            grouped = x_pool.tile([P, PASSES * N_MOVE * PACK], BF16, align_bytes=64, tag="x_grouped", bufs=HALVES)
+            grouped_words = grouped[:].bitcast(F32).rearrange("p (g t u) -> p g t u", g=PASSES, u=WORDS)
+            for a in range(TILES_PER_HALF):
+                words = x_raw[(half, a)][:].bitcast(F32).rearrange("p (g q u) -> p g u q", g=PASSES, u=WORDS)
+                transposed = psum.tile([P, PASSES, WORDS, P], F32, tag="transposed")
+                for g, u in product(range(PASSES), range(WORDS)):
+                    nc.tensor.transpose(out=transposed[:, g, u, :], in_=words[:, g, u, :], identity=ident[:])
+                nc.scalar.copy(
+                    out=grouped_words[:, :, a * P : (a + 1) * P, :],
+                    in_=transposed[:].rearrange("p g u t -> p g t u"),
+                )
+            for g in range(PASSES):
+                codes = x_pool.tile([P, N_MOVE], U32, align_bytes=64, tag="x_codes", bufs=HALVES * PASSES)
+                scales = x_pool.tile([P, N_MOVE], U8, align_bytes=64, tag="x_scales", bufs=HALVES * PASSES)
+                nc.vector.quantize_mx(
+                    out=codes[:].bitcast(FP8X4),
+                    scales=scales[:],
+                    in_=grouped[:, g * N_MOVE * PACK : (g + 1) * N_MOVE * PACK],
+                )
+                x_quant[(g, half)] = (codes, scales)
+
+        w_grouped = {}
+        w_quant = {}
+
+        def regroup_weight_piece(w, g, c):
+            grouped = group_pool.tile([P, CHUNK, PACK], BF16, align_bytes=64, tag="w_grouped")
+            src = w_raw[(w, g, c)][:].rearrange("p j (c i) -> p c j i", i=RUN)
+            dst = grouped[:].rearrange("p (c i) j -> p c j i", i=RUN)
+            split = VECTOR_COLS // RUN
+            nc.vector.tensor_copy(out=dst[:, :split], in_=src[:, :split])
+            nc.scalar.copy(out=dst[:, split:], in_=src[:, split:])
+            w_grouped[(w, g, c)] = grouped
+
+        def quantise_weight_piece(w, g, c):
+            codes = w_pool.tile([P, CHUNK], U32, align_bytes=64, tag="w_codes")
+            scales = w_pool.tile([P, CHUNK], U8, align_bytes=64, tag="w_scales")
+            nc.vector.quantize_mx(
+                out=codes[:].bitcast(FP8X4),
+                scales=scales[:],
+                in_=w_grouped[(w, g, c)][:].rearrange("p c j -> p (c j)"),
+            )
+            w_quant[(w, g, c)] = (codes, scales)
+
+        def multiply(w, t, half, acc):
+            c, local = divmod(t, TILES_PER_CHUNK)
+            cols = slice(local * P, (local + 1) * P)
+            for g in range(PASSES):
+                w_codes, w_scales = w_quant[(w, g, c)]
+                x_codes, x_scales = x_quant[(g, half)]
+                nc.tensor.matmul_mx(
+                    out=acc[:],
+                    lhsT=w_codes[:, cols].bitcast(FP8X4),
+                    lhsT_scale=w_scales[:, cols],
+                    rhs=x_codes[:].bitcast(FP8X4),
+                    rhs_scale=x_scales[:],
+                    start=(g == 0),
+                    stop=(g == PASSES - 1),
+                )
+
+        def attend(t, half):
+            key_acc = psum.tile([P, N_MOVE], F32, tag="key_acc", bufs=3)
+            multiply(0, t, half, key_acc)
+            value_acc = psum.tile([P, N_MOVE], F32, tag="value_acc", bufs=3)
+            multiply(1, t, half, value_acc)
+
+            exp_v = work.tile([P, N_MOVE], F32, tag="exp_v")
+            nc.scalar.activation(out=exp_v[:], in_=key_acc[:], func=ACT.Exp, bias=bias_cols[:, t : t + 1])
+            v_plus_1 = work.tile([P, N_MOVE], F32, tag="v_plus_1")
+            nc.scalar.activation(out=v_plus_1[:], in_=key_acc[:], func=ACT.Identity, bias=bk_plus_1[:, t : t + 1])
+
+            k_feat = work.tile([P, N_MOVE], F32, tag="k_feat")
+            k_value = work.tile([P, N_MOVE], F32, tag="k_value")
+            for b in range(BATCHES_PER_HALF):
+                n = half * BATCHES_PER_HALF + b
+                toks = slice(b * SEQ, (b + 1) * SEQ)
+                ksum_col = BATCHES * H_TILES + n * H_TILES + t
+                nc.vector.scalar_tensor_tensor(
+                    out=k_feat[:, toks],
+                    in0=exp_v[:, toks],
+                    scalar=1.0,
+                    in1=v_plus_1[:, toks],
+                    op0=ALU.min,
+                    op1=ALU.max,
+                    accum_out=sums[:, ksum_col : ksum_col + 1],
+                )
+            for b in range(BATCHES_PER_HALF):
+                n = half * BATCHES_PER_HALF + b
+                toks = slice(b * SEQ, (b + 1) * SEQ)
+                kv_col = n * H_TILES + t
+                nc.vector.scalar_tensor_tensor(
+                    out=k_value[:, toks],
+                    in0=value_acc[:, toks],
+                    scalar=bias_cols[:, H_TILES + t : H_TILES + t + 1],
+                    in1=k_feat[:, toks],
+                    op0=ALU.add,
+                    op1=ALU.mult,
+                    accum_out=sums[:, kv_col : kv_col + 1],
+                )
+
+        pieces = list(product(range(WEIGHTS), range(PASSES)))
+
+        prepare_x_half(0)
+        for w, g in pieces:
+            regroup_weight_piece(w, g, 0)
+        for w, g in pieces:
+            quantise_weight_piece(w, g, 0)
+
+        for c in range(CHUNKS):
+            units = list(product(range(HALVES), range(TILES_PER_CHUNK)))
+            for (half, local), (w, g) in zip(units, pieces):
+                if (0, half) not in x_quant:
+                    prepare_x_half(half)
+                if c + 1 < CHUNKS:
+                    regroup_weight_piece(w, g, c + 1)
+                attend(c * TILES_PER_CHUNK + local, half)
+                if c + 1 < CHUNKS:
+                    quantise_weight_piece(w, g, c + 1)
+
+        sums_ps = psum.tile([P, P], F32, tag="transposed")
+        nc.tensor.transpose(out=sums_ps[:], in_=sums[:], identity=ident[:])
+        result = consts.tile([P, P], F32)
+        nc.vector.tensor_copy(out=result[:], in_=sums_ps[:])
+        rows = BATCHES * H_TILES
+        nc.sync.dma_start(out=out_0.rearrange("n (t p) -> (n t) p", p=P), in_=result[0:rows, :])
+        nc.scalar.dma_start(out=out_1.rearrange("n (t p) -> (n t) p", p=P), in_=result[rows : 2 * rows, :])

@@ -23,6 +23,7 @@ WORDS = PACK // 2
 
 N_MOVE = 512
 HALVES = TOKENS // N_MOVE
+TOKEN_TILES = TOKENS // P
 TILES_PER_HALF = N_MOVE // P
 BATCHES_PER_HALF = N_MOVE // SEQ
 
@@ -32,9 +33,15 @@ CHUNKS = H // CHUNK
 TILES_PER_CHUNK = CHUNK // P
 WEIGHTS = 2
 PIECES = WEIGHTS * PASSES * CHUNKS
+KEY, VALUE = 0, 1
+
+UNITS = H_TILES * HALVES
+UNITS_PER_CHUNK = TILES_PER_CHUNK * HALVES
 
 RUN = 4
-VECTOR_COLS = 128
+
+KEYS_AHEAD = 2
+EXP_AHEAD = 1
 
 FLOPS = 2 * WEIGHTS * TOKENS * D * H
 
@@ -45,39 +52,36 @@ def tile_linearattention_pa_kernel(tc, x, Wk, bk, Wv, bv, out_0, out_1):
     weights = (Wk, Wv)
 
     with ExitStack() as ctx:
+        ctx.enter_context(tc.manual_schedule())
         consts = ctx.enter_context(tc.tile_pool(name="consts", bufs=1))
         x_pool = ctx.enter_context(tc.tile_pool(name="x_pool", bufs=1))
         w_pool = ctx.enter_context(tc.tile_pool(name="w_pool", bufs=PIECES))
-        group_pool = ctx.enter_context(tc.tile_pool(name="group_pool", bufs=4))
+        group_pool = ctx.enter_context(tc.tile_pool(name="group_pool", bufs=2))
         work = ctx.enter_context(tc.tile_pool(name="work", bufs=3))
-        psum = ctx.enter_context(tc.psum_pool(name="psum", bufs=2))
+        psum = ctx.enter_context(tc.psum_pool(name="psum", bufs=4))
+        bank_tags = ("key_acc", "value_acc")
+
+        bias_rows = consts.tile([P, P], BF16)
+        nc.vector.memset(bias_rows[:], 0.0)
+        nc.scalar.dma_start(out=bias_rows[0:H_TILES, :], in_=bk.rearrange("(t p) -> t p", p=P))
+        nc.scalar.dma_start(out=bias_rows[H_TILES : 2 * H_TILES, :], in_=bv.rearrange("(t p) -> t p", p=P))
 
         x_raw = {}
+        for a in range(TOKEN_TILES):
+            raw = x_pool.tile([P, D], BF16, tag="x_raw", bufs=TOKEN_TILES)
+            nc.sync.dma_start(out=raw[:], in_=x_rows[a * P : (a + 1) * P, :])
+            x_raw[a] = raw
+
         w_raw = {}
-
-        def load_x_half(half):
-            for a in range(TILES_PER_HALF):
-                tokens = slice((half * TILES_PER_HALF + a) * P, (half * TILES_PER_HALF + a + 1) * P)
-                raw = x_pool.tile([P, D], BF16, tag="x_raw", bufs=HALVES * TILES_PER_HALF)
-                nc.sync.dma_start(out=raw[:], in_=x_rows[tokens, :])
-                x_raw[(half, a)] = raw
-
-        def load_weight_chunk(c):
-            for w, g in product(range(WEIGHTS), range(PASSES)):
-                raw = w_pool.tile([P, PACK, CHUNK], BF16, tag="w_raw")
-                nc.sync.dma_start(
-                    out=raw[:],
-                    in_=weights[w][g * K_PASS : (g + 1) * K_PASS, c * CHUNK : (c + 1) * CHUNK].rearrange(
-                        "(p j) c -> p j c", j=PACK
-                    ),
-                )
-                w_raw[(w, g, c)] = raw
-
-        load_x_half(0)
-        load_weight_chunk(0)
-        load_x_half(1)
-        for c in range(1, CHUNKS):
-            load_weight_chunk(c)
+        for c, w, g in product(range(CHUNKS), range(WEIGHTS), range(PASSES)):
+            raw = w_pool.tile([P, PACK, CHUNK], BF16, tag="w_raw")
+            nc.sync.dma_start(
+                out=raw[:],
+                in_=weights[w][g * K_PASS : (g + 1) * K_PASS, c * CHUNK : (c + 1) * CHUNK].rearrange(
+                    "(p j) c -> p j c", j=PACK
+                ),
+            )
+            w_raw[(c, w, g)] = raw
 
         ident = consts.tile([P, P], F32)
         make_identity(nc, ident[:])
@@ -86,144 +90,203 @@ def tile_linearattention_pa_kernel(tc, x, Wk, bk, Wv, bv, out_0, out_1):
         nc.vector.memset(warm[:], 0.0)
         nc.scalar.activation(out=warm[:], in_=warm[:], func=ACT.Exp)
 
-        bias_rows = consts.tile([P, P], BF16)
-        nc.vector.memset(bias_rows[:], 0.0)
-        nc.scalar.dma_start(out=bias_rows[0:H_TILES, :], in_=bk.rearrange("(t p) -> t p", p=P))
-        nc.scalar.dma_start(out=bias_rows[H_TILES : 2 * H_TILES, :], in_=bv.rearrange("(t p) -> t p", p=P))
-        bias_rows_f32 = consts.tile([P, P], F32)
-        nc.vector.tensor_copy(out=bias_rows_f32[:], in_=bias_rows[:])
-        bias_ps = psum.tile([P, P], F32, tag="transposed")
-        nc.tensor.transpose(out=bias_ps[:], in_=bias_rows_f32[:], identity=ident[:])
-        bias_cols = consts.tile([P, 2 * H_TILES], F32)
-        nc.vector.tensor_copy(out=bias_cols[:], in_=bias_ps[:, 0 : 2 * H_TILES])
-        bk_plus_1 = consts.tile([P, H_TILES], F32)
-        nc.vector.tensor_scalar_add(out=bk_plus_1[:], in0=bias_ps[:, 0:H_TILES], scalar1=1.0)
-
         sums = consts.tile([P, P], F32)
         nc.vector.memset(sums[:], 0.0)
 
+        x_grouped = {}
         x_quant = {}
 
-        def prepare_x_half(half):
+        def transpose_x_half(half):
             grouped = x_pool.tile([P, PASSES * N_MOVE * PACK], BF16, align_bytes=64, tag="x_grouped", bufs=HALVES)
             grouped_words = grouped[:].bitcast(F32).rearrange("p (g t u) -> p g t u", g=PASSES, u=WORDS)
             for a in range(TILES_PER_HALF):
-                words = x_raw[(half, a)][:].bitcast(F32).rearrange("p (g q u) -> p g u q", g=PASSES, u=WORDS)
-                transposed = psum.tile([P, PASSES, WORDS, P], F32, tag="transposed")
+                words = (
+                    x_raw[half * TILES_PER_HALF + a][:]
+                    .bitcast(F32)
+                    .rearrange("p (g q u) -> p g u q", g=PASSES, u=WORDS)
+                )
+                transposed = psum.tile([P, PASSES, WORDS, P], F32, tag=bank_tags[a % 2])
                 for g, u in product(range(PASSES), range(WORDS)):
                     nc.tensor.transpose(out=transposed[:, g, u, :], in_=words[:, g, u, :], identity=ident[:])
                 nc.scalar.copy(
                     out=grouped_words[:, :, a * P : (a + 1) * P, :],
                     in_=transposed[:].rearrange("p g u t -> p g t u"),
                 )
+            x_grouped[half] = grouped
+
+        def quantise_x_half(half):
             for g in range(PASSES):
                 codes = x_pool.tile([P, N_MOVE], U32, align_bytes=64, tag="x_codes", bufs=HALVES * PASSES)
                 scales = x_pool.tile([P, N_MOVE], U8, align_bytes=64, tag="x_scales", bufs=HALVES * PASSES)
                 nc.vector.quantize_mx(
                     out=codes[:].bitcast(FP8X4),
                     scales=scales[:],
-                    in_=grouped[:, g * N_MOVE * PACK : (g + 1) * N_MOVE * PACK],
+                    in_=x_grouped[half][:, g * N_MOVE * PACK : (g + 1) * N_MOVE * PACK],
                 )
                 x_quant[(g, half)] = (codes, scales)
 
         w_grouped = {}
         w_quant = {}
 
-        def regroup_weight_piece(w, g, c):
-            grouped = group_pool.tile([P, CHUNK, PACK], BF16, align_bytes=64, tag="w_grouped")
-            src = w_raw[(w, g, c)][:].rearrange("p j (c i) -> p c j i", i=RUN)
-            dst = grouped[:].rearrange("p (c i) j -> p c j i", i=RUN)
-            split = VECTOR_COLS // RUN
-            nc.vector.tensor_copy(out=dst[:, :split], in_=src[:, :split])
-            nc.scalar.copy(out=dst[:, split:], in_=src[:, split:])
-            w_grouped[(w, g, c)] = grouped
+        def regroup_weight_piece(c, w, g, engine):
+            if g == 0:
+                w_grouped[(c, w)] = group_pool.tile(
+                    [P, PASSES, CHUNK, PACK],
+                    BF16,
+                    align_bytes=64,
+                    name="w_grouped",
+                    tag="grouped_by_" + engine,
+                    bufs=1 if engine == "gpsimd" else 2,
+                )
+            grouped = w_grouped[(c, w)][:, g]
+            raw = w_raw[(c, w, g)][:]
+            if engine == "gpsimd":
+                nc.gpsimd.tensor_scalar(
+                    out=grouped,
+                    in0=raw.rearrange("p j c -> p c j"),
+                    scalar1=1.0,
+                    scalar2=0.0,
+                    op0=ALU.mult,
+                    op1=ALU.add,
+                )
+            else:
+                copy = nc.vector.tensor_copy if engine == "vector" else nc.scalar.copy
+                copy(
+                    out=grouped.rearrange("p (c i) j -> p c j i", i=RUN),
+                    in_=raw.rearrange("p j (c i) -> p c j i", i=RUN),
+                )
 
-        def quantise_weight_piece(w, g, c):
-            codes = w_pool.tile([P, CHUNK], U32, align_bytes=64, tag="w_codes")
-            scales = w_pool.tile([P, CHUNK], U8, align_bytes=64, tag="w_scales")
+        def quantise_weight_chunk(c, w):
+            codes = w_pool.tile([P, PASSES, CHUNK], U32, align_bytes=64, tag="w_codes", bufs=WEIGHTS * CHUNKS)
+            scales = w_pool.tile([P, PASSES, CHUNK], U8, align_bytes=64, tag="w_scales", bufs=WEIGHTS * CHUNKS)
             nc.vector.quantize_mx(
-                out=codes[:].bitcast(FP8X4),
-                scales=scales[:],
-                in_=w_grouped[(w, g, c)][:].rearrange("p c j -> p (c j)"),
+                out=codes[:].rearrange("p g c -> p (g c)").bitcast(FP8X4),
+                scales=scales[:].rearrange("p g c -> p (g c)"),
+                in_=w_grouped[(c, w)][:].rearrange("p g c j -> p (g c j)"),
             )
-            w_quant[(w, g, c)] = (codes, scales)
+            w_quant[(c, w)] = (codes, scales)
 
-        def multiply(w, t, half, acc):
-            c, local = divmod(t, TILES_PER_CHUNK)
+        def unit_place(i):
+            c, rest = divmod(i, UNITS_PER_CHUNK)
+            half, local = divmod(rest, TILES_PER_CHUNK)
+            return c, local, half
+
+        def multiply(w, i, acc):
+            c, local, half = unit_place(i)
             cols = slice(local * P, (local + 1) * P)
+            w_codes, w_scales = w_quant[(c, w)]
             for g in range(PASSES):
-                w_codes, w_scales = w_quant[(w, g, c)]
                 x_codes, x_scales = x_quant[(g, half)]
                 nc.tensor.matmul_mx(
                     out=acc[:],
-                    lhsT=w_codes[:, cols].bitcast(FP8X4),
-                    lhsT_scale=w_scales[:, cols],
+                    lhsT=w_codes[:, g, cols].bitcast(FP8X4),
+                    lhsT_scale=w_scales[:, g, cols],
                     rhs=x_codes[:].bitcast(FP8X4),
                     rhs_scale=x_scales[:],
                     start=(g == 0),
                     stop=(g == PASSES - 1),
                 )
 
-        def attend(t, half):
-            key_acc = psum.tile([P, N_MOVE], F32, tag="key_acc", bufs=3)
-            multiply(0, t, half, key_acc)
-            value_acc = psum.tile([P, N_MOVE], F32, tag="value_acc", bufs=3)
-            multiply(1, t, half, value_acc)
+        key_acc = {}
+        value_acc = {}
+        relu_minus_v = {}
+        exp_min_v_0 = {}
 
-            exp_v = work.tile([P, N_MOVE], F32, tag="exp_v")
-            nc.scalar.activation(out=exp_v[:], in_=key_acc[:], func=ACT.Exp, bias=bias_cols[:, t : t + 1])
-            v_plus_1 = work.tile([P, N_MOVE], F32, tag="v_plus_1")
-            nc.scalar.activation(out=v_plus_1[:], in_=key_acc[:], func=ACT.Identity, bias=bk_plus_1[:, t : t + 1])
+        def stage_keys(i):
+            c, local, half = unit_place(i)
+            t = c * TILES_PER_CHUNK + local
+            key_acc[i] = psum.tile([P, N_MOVE], F32, tag="key_acc", name="key_acc")
+            multiply(KEY, i, key_acc[i])
+            relu_minus_v[i] = work.tile([P, N_MOVE], F32, tag="relu_minus_v", name="relu_minus_v")
+            nc.scalar.activation(
+                out=relu_minus_v[i][:], in_=key_acc[i][:], func=ACT.Relu, scale=-1.0, bias=minus_bk[:, t : t + 1]
+            )
 
+        def stage_exp(i):
+            exp_min_v_0[i] = work.tile([P, N_MOVE], F32, tag="exp_min_v_0", name="exp_min_v_0")
+            nc.scalar.activation(out=exp_min_v_0[i][:], in_=relu_minus_v[i][:], func=ACT.Exp, scale=-1.0)
+
+        def stage_values(i):
+            value_acc[i] = psum.tile([P, N_MOVE], F32, tag="value_acc", name="value_acc")
+            multiply(VALUE, i, value_acc[i])
+
+        def stage_sums(i):
+            c, local, half = unit_place(i)
+            t = c * TILES_PER_CHUNK + local
             k_feat = work.tile([P, N_MOVE], F32, tag="k_feat")
             k_value = work.tile([P, N_MOVE], F32, tag="k_value")
             for b in range(BATCHES_PER_HALF):
-                n = half * BATCHES_PER_HALF + b
                 toks = slice(b * SEQ, (b + 1) * SEQ)
-                ksum_col = BATCHES * H_TILES + n * H_TILES + t
+                ksum_col = BATCHES * H_TILES + (half * BATCHES_PER_HALF + b) * H_TILES + t
                 nc.vector.scalar_tensor_tensor(
                     out=k_feat[:, toks],
-                    in0=exp_v[:, toks],
-                    scalar=1.0,
-                    in1=v_plus_1[:, toks],
-                    op0=ALU.min,
+                    in0=key_acc[i][:, toks],
+                    scalar=bk_plus_1[:, t : t + 1],
+                    in1=exp_min_v_0[i][:, toks],
+                    op0=ALU.add,
                     op1=ALU.max,
                     accum_out=sums[:, ksum_col : ksum_col + 1],
                 )
             for b in range(BATCHES_PER_HALF):
-                n = half * BATCHES_PER_HALF + b
                 toks = slice(b * SEQ, (b + 1) * SEQ)
-                kv_col = n * H_TILES + t
+                kv_col = (half * BATCHES_PER_HALF + b) * H_TILES + t
                 nc.vector.scalar_tensor_tensor(
                     out=k_value[:, toks],
-                    in0=value_acc[:, toks],
-                    scalar=bias_cols[:, H_TILES + t : H_TILES + t + 1],
+                    in0=value_acc[i][:, toks],
+                    scalar=bv_cols[:, t : t + 1],
                     in1=k_feat[:, toks],
                     op0=ALU.add,
                     op1=ALU.mult,
                     accum_out=sums[:, kv_col : kv_col + 1],
                 )
 
-        pieces = list(product(range(WEIGHTS), range(PASSES)))
+        transpose_x_half(0)
 
-        prepare_x_half(0)
-        for w, g in pieces:
-            regroup_weight_piece(w, g, 0)
-        for w, g in pieces:
-            quantise_weight_piece(w, g, 0)
+        bias_rows_f32 = consts.tile([P, P], F32)
+        nc.vector.tensor_copy(out=bias_rows_f32[:], in_=bias_rows[:])
+        bias_ps = psum.tile([P, P], F32, tag="key_acc")
+        nc.tensor.transpose(out=bias_ps[:], in_=bias_rows_f32[:], identity=ident[:])
+        bv_cols = consts.tile([P, H_TILES], F32)
+        nc.vector.tensor_copy(out=bv_cols[:], in_=bias_ps[:, H_TILES : 2 * H_TILES])
+        bk_plus_1 = consts.tile([P, H_TILES], F32)
+        nc.vector.tensor_scalar_add(out=bk_plus_1[:], in0=bias_ps[:, 0:H_TILES], scalar1=1.0)
+        minus_bk = consts.tile([P, H_TILES], F32)
+        nc.vector.tensor_scalar_mul(out=minus_bk[:], in0=bias_ps[:, 0:H_TILES], scalar1=-1.0)
 
-        for c in range(CHUNKS):
-            units = list(product(range(HALVES), range(TILES_PER_CHUNK)))
-            for (half, local), (w, g) in zip(units, pieces):
-                if (0, half) not in x_quant:
-                    prepare_x_half(half)
-                if c + 1 < CHUNKS:
-                    regroup_weight_piece(w, g, c + 1)
-                attend(c * TILES_PER_CHUNK + local, half)
-                if c + 1 < CHUNKS:
-                    quantise_weight_piece(w, g, c + 1)
+        quantise_x_half(0)
+        transpose_x_half(1)
+        for w in (KEY, VALUE):
+            for g in range(PASSES):
+                regroup_weight_piece(0, w, g, "vector")
+            quantise_weight_chunk(0, w)
+        quantise_x_half(1)
 
-        sums_ps = psum.tile([P, P], F32, tag="transposed")
+        for g in range(PASSES):
+            regroup_weight_piece(1, KEY, g, "gpsimd")
+
+        for i in range(-KEYS_AHEAD, UNITS):
+            if 0 <= i + EXP_AHEAD < UNITS:
+                stage_exp(i + EXP_AHEAD)
+            if i + KEYS_AHEAD < UNITS:
+                stage_keys(i + KEYS_AHEAD)
+            if 0 <= i + EXP_AHEAD < UNITS:
+                stage_values(i + EXP_AHEAD)
+            if i < 0:
+                continue
+            c, place_in_chunk = divmod(i, UNITS_PER_CHUNK)
+            more_chunks = c + 1 < CHUNKS
+            if more_chunks and place_in_chunk < PASSES:
+                regroup_weight_piece(c + 1, VALUE, place_in_chunk, "scalar")
+            stage_sums(i)
+            if more_chunks and place_in_chunk == UNITS_PER_CHUNK - KEYS_AHEAD - 1:
+                quantise_weight_chunk(c + 1, KEY)
+                if c + 2 < CHUNKS:
+                    for g in range(PASSES):
+                        regroup_weight_piece(c + 2, KEY, g, "gpsimd")
+            if more_chunks and place_in_chunk == UNITS_PER_CHUNK - EXP_AHEAD - 1:
+                quantise_weight_chunk(c + 1, VALUE)
+
+        sums_ps = psum.tile([P, P], F32, tag="key_acc")
         nc.tensor.transpose(out=sums_ps[:], in_=sums[:], identity=ident[:])
         result = consts.tile([P, P], F32)
         nc.vector.tensor_copy(out=result[:], in_=sums_ps[:])

@@ -43,6 +43,8 @@ RUN = 4
 KEYS_AHEAD = 2
 EXP_AHEAD = 1
 
+GPSIMD_PIECES = 3
+
 FLOPS = 2 * WEIGHTS * TOKENS * D * H
 
 
@@ -56,7 +58,7 @@ def tile_linearattention_pa_kernel(tc, x, Wk, bk, Wv, bv, out_0, out_1):
         consts = ctx.enter_context(tc.tile_pool(name="consts", bufs=1))
         x_pool = ctx.enter_context(tc.tile_pool(name="x_pool", bufs=1))
         w_pool = ctx.enter_context(tc.tile_pool(name="w_pool", bufs=PIECES))
-        group_pool = ctx.enter_context(tc.tile_pool(name="group_pool", bufs=2))
+        group_pool = ctx.enter_context(tc.tile_pool(name="group_pool", bufs=1))
         work = ctx.enter_context(tc.tile_pool(name="work", bufs=3))
         psum = ctx.enter_context(tc.psum_pool(name="psum", bufs=4))
         bank_tags = ("key_acc", "value_acc")
@@ -129,16 +131,11 @@ def tile_linearattention_pa_kernel(tc, x, Wk, bk, Wv, bv, out_0, out_1):
         w_quant = {}
 
         def regroup_weight_piece(c, w, g, engine):
-            if g == 0:
-                w_grouped[(c, w)] = group_pool.tile(
-                    [P, PASSES, CHUNK, PACK],
-                    BF16,
-                    align_bytes=64,
-                    name="w_grouped",
-                    tag="grouped_by_" + engine,
-                    bufs=1 if engine == "gpsimd" else 2,
+            if c not in w_grouped:
+                w_grouped[c] = group_pool.tile(
+                    [P, WEIGHTS, PASSES, CHUNK, PACK], BF16, align_bytes=64, name="w_grouped", tag="w_grouped"
                 )
-            grouped = w_grouped[(c, w)][:, g]
+            grouped = w_grouped[c][:, w, g]
             raw = w_raw[(c, w, g)][:]
             if engine == "gpsimd":
                 nc.gpsimd.tensor_scalar(
@@ -162,7 +159,7 @@ def tile_linearattention_pa_kernel(tc, x, Wk, bk, Wv, bv, out_0, out_1):
             nc.vector.quantize_mx(
                 out=codes[:].rearrange("p g c -> p (g c)").bitcast(FP8X4),
                 scales=scales[:].rearrange("p g c -> p (g c)"),
-                in_=w_grouped[(c, w)][:].rearrange("p g c j -> p (g c j)"),
+                in_=w_grouped[c][:, w].rearrange("p g c j -> p (g c j)"),
             )
             w_quant[(c, w)] = (codes, scales)
 
@@ -255,14 +252,17 @@ def tile_linearattention_pa_kernel(tc, x, Wk, bk, Wv, bv, out_0, out_1):
 
         quantise_x_half(0)
         transpose_x_half(1)
-        for w in (KEY, VALUE):
-            for g in range(PASSES):
-                regroup_weight_piece(0, w, g, "vector")
-            quantise_weight_chunk(0, w)
-        quantise_x_half(1)
-
         for g in range(PASSES):
-            regroup_weight_piece(1, KEY, g, "gpsimd")
+            regroup_weight_piece(0, KEY, g, "vector")
+        quantise_weight_chunk(0, KEY)
+        for g in range(PASSES):
+            regroup_weight_piece(0, VALUE, g, "vector")
+        quantise_x_half(1)
+        quantise_weight_chunk(0, VALUE)
+
+        pieces = list(product(range(WEIGHTS), range(PASSES)))
+        for w, g in pieces[:GPSIMD_PIECES]:
+            regroup_weight_piece(1, w, g, "gpsimd")
 
         for i in range(-KEYS_AHEAD, UNITS):
             if 0 <= i + EXP_AHEAD < UNITS:
@@ -275,16 +275,15 @@ def tile_linearattention_pa_kernel(tc, x, Wk, bk, Wv, bv, out_0, out_1):
                 continue
             c, place_in_chunk = divmod(i, UNITS_PER_CHUNK)
             more_chunks = c + 1 < CHUNKS
-            if more_chunks and place_in_chunk < PASSES:
-                regroup_weight_piece(c + 1, VALUE, place_in_chunk, "scalar")
+            if more_chunks and place_in_chunk < len(pieces) - GPSIMD_PIECES:
+                regroup_weight_piece(c + 1, *pieces[GPSIMD_PIECES + place_in_chunk], "scalar")
             stage_sums(i)
             if more_chunks and place_in_chunk == UNITS_PER_CHUNK - KEYS_AHEAD - 1:
                 quantise_weight_chunk(c + 1, KEY)
-                if c + 2 < CHUNKS:
-                    for g in range(PASSES):
-                        regroup_weight_piece(c + 2, KEY, g, "gpsimd")
-            if more_chunks and place_in_chunk == UNITS_PER_CHUNK - EXP_AHEAD - 1:
                 quantise_weight_chunk(c + 1, VALUE)
+                if c + 2 < CHUNKS:
+                    for w, g in pieces[:GPSIMD_PIECES]:
+                        regroup_weight_piece(c + 2, w, g, "gpsimd")
 
         sums_ps = psum.tile([P, P], F32, tag="key_acc")
         nc.tensor.transpose(out=sums_ps[:], in_=sums[:], identity=ident[:])
@@ -292,4 +291,4 @@ def tile_linearattention_pa_kernel(tc, x, Wk, bk, Wv, bv, out_0, out_1):
         nc.vector.tensor_copy(out=result[:], in_=sums_ps[:])
         rows = BATCHES * H_TILES
         nc.sync.dma_start(out=out_0.rearrange("n (t p) -> (n t) p", p=P), in_=result[0:rows, :])
-        nc.scalar.dma_start(out=out_1.rearrange("n (t p) -> (n t) p", p=P), in_=result[rows : 2 * rows, :])
+        nc.sync.dma_start(out=out_1.rearrange("n (t p) -> (n t) p", p=P), in_=result[rows : 2 * rows, :])

@@ -69,21 +69,31 @@ def tile_linearattention_pa_kernel(tc, x, Wk, bk, Wv, bv, out_0, out_1):
         nc.scalar.dma_start(out=bias_rows[H_TILES : 2 * H_TILES, :], in_=bv.rearrange("(t p) -> t p", p=P))
 
         x_raw = {}
-        for a in range(TOKEN_TILES):
-            raw = x_pool.tile([P, D], BF16, tag="x_raw", bufs=TOKEN_TILES)
-            nc.sync.dma_start(out=raw[:], in_=x_rows[a * P : (a + 1) * P, :])
-            x_raw[a] = raw
-
         w_raw = {}
-        for c, w, g in product(range(CHUNKS), range(WEIGHTS), range(PASSES)):
-            raw = w_pool.tile([P, PACK, CHUNK], BF16, tag="w_raw")
-            nc.sync.dma_start(
-                out=raw[:],
-                in_=weights[w][g * K_PASS : (g + 1) * K_PASS, c * CHUNK : (c + 1) * CHUNK].rearrange(
-                    "(p j) c -> p j c", j=PACK
-                ),
-            )
-            w_raw[(c, w, g)] = raw
+
+        def load_x_half(half):
+            for a in range(half * TILES_PER_HALF, (half + 1) * TILES_PER_HALF):
+                raw = x_pool.tile([P, D], BF16, tag="x_raw", bufs=TOKEN_TILES)
+                nc.sync.dma_start(out=raw[:], in_=x_rows[a * P : (a + 1) * P, :])
+                x_raw[a] = raw
+
+        def load_weight_chunk(c, w):
+            for g in range(PASSES):
+                raw = w_pool.tile([P, PACK, CHUNK], BF16, tag="w_raw")
+                nc.sync.dma_start(
+                    out=raw[:],
+                    in_=weights[w][g * K_PASS : (g + 1) * K_PASS, c * CHUNK : (c + 1) * CHUNK].rearrange(
+                        "(p j) c -> p j c", j=PACK
+                    ),
+                )
+                w_raw[(c, w, g)] = raw
+
+        load_x_half(0)
+        load_weight_chunk(0, KEY)
+        load_x_half(1)
+        load_weight_chunk(0, VALUE)
+        for c, w in product(range(1, CHUNKS), range(WEIGHTS)):
+            load_weight_chunk(c, w)
 
         ident = consts.tile([P, P], F32)
         make_identity(nc, ident[:])
@@ -250,15 +260,15 @@ def tile_linearattention_pa_kernel(tc, x, Wk, bk, Wv, bv, out_0, out_1):
         minus_bk = consts.tile([P, H_TILES], F32)
         nc.vector.tensor_scalar_mul(out=minus_bk[:], in0=bias_ps[:, 0:H_TILES], scalar1=-1.0)
 
-        quantise_x_half(0)
-        transpose_x_half(1)
         for g in range(PASSES):
             regroup_weight_piece(0, KEY, g, "vector")
+        quantise_x_half(0)
         quantise_weight_chunk(0, KEY)
+        transpose_x_half(1)
         for g in range(PASSES):
             regroup_weight_piece(0, VALUE, g, "vector")
-        quantise_x_half(1)
         quantise_weight_chunk(0, VALUE)
+        quantise_x_half(1)
 
         pieces = list(product(range(WEIGHTS), range(PASSES)))
         for w, g in pieces[:GPSIMD_PIECES]:
@@ -280,6 +290,7 @@ def tile_linearattention_pa_kernel(tc, x, Wk, bk, Wv, bv, out_0, out_1):
             stage_sums(i)
             if more_chunks and place_in_chunk == UNITS_PER_CHUNK - KEYS_AHEAD - 1:
                 quantise_weight_chunk(c + 1, KEY)
+            if more_chunks and place_in_chunk == UNITS_PER_CHUNK - EXP_AHEAD - 1:
                 quantise_weight_chunk(c + 1, VALUE)
                 if c + 2 < CHUNKS:
                     for w, g in pieces[:GPSIMD_PIECES]:

@@ -38,7 +38,7 @@ KEY, VALUE = 0, 1
 UNITS = H_TILES * HALVES
 UNITS_PER_CHUNK = TILES_PER_CHUNK * HALVES
 
-RUN = 4
+RUN = 8
 
 KEYS_AHEAD = 2
 EXP_AHEAD = 1

from contextlib import ExitStack
from itertools import product

import concourse.mybir as mybir
from concourse.masks import make_identity

F32 = mybir.dt.float32
BF16 = mybir.dt.bfloat16
U32 = mybir.dt.uint32
U8 = mybir.dt.uint8
FP8X4 = mybir.dt.float8_e4m3fn_x4
ALU = mybir.AluOpType
ACT = mybir.ActivationFunctionType

BATCHES, SEQ, D, H = 4, 256, 1024, 1024
TOKENS = BATCHES * SEQ

P = 128
PACK = 4
K_PASS = P * PACK
PASSES = D // K_PASS
WORDS = PACK // 2

N_MOVE = 512
HALVES = TOKENS // N_MOVE
TOKEN_TILES = TOKENS // P
TILES_PER_HALF = N_MOVE // P
BATCHES_PER_HALF = N_MOVE // SEQ

H_TILES = H // P
CHUNK = 256
CHUNKS = H // CHUNK
TILES_PER_CHUNK = CHUNK // P
WEIGHTS = 2
PIECES = WEIGHTS * PASSES * CHUNKS
KEY, VALUE = 0, 1

UNITS = H_TILES * HALVES
UNITS_PER_CHUNK = TILES_PER_CHUNK * HALVES

RUN = 8

KEYS_AHEAD = 2
EXP_AHEAD = 1

GPSIMD_PIECES = 3

FLOPS = 2 * WEIGHTS * TOKENS * D * H


def tile_linearattention_pa_kernel(tc, x, Wk, bk, Wv, bv, out_0, out_1):
    nc = tc.nc
    x_rows = x.rearrange("n s d -> (n s) d")
    weights = (Wk, Wv)

    with ExitStack() as ctx:
        ctx.enter_context(tc.manual_schedule())
        consts = ctx.enter_context(tc.tile_pool(name="consts", bufs=1))
        x_pool = ctx.enter_context(tc.tile_pool(name="x_pool", bufs=1))
        w_pool = ctx.enter_context(tc.tile_pool(name="w_pool", bufs=PIECES))
        group_pool = ctx.enter_context(tc.tile_pool(name="group_pool", bufs=1))
        work = ctx.enter_context(tc.tile_pool(name="work", bufs=3))
        psum = ctx.enter_context(tc.psum_pool(name="psum", bufs=4))
        bank_tags = ("key_acc", "value_acc")

        bias_rows = consts.tile([P, P], BF16)
        nc.vector.memset(bias_rows[:], 0.0)
        nc.scalar.dma_start(out=bias_rows[0:H_TILES, :], in_=bk.rearrange("(t p) -> t p", p=P))
        nc.scalar.dma_start(out=bias_rows[H_TILES : 2 * H_TILES, :], in_=bv.rearrange("(t p) -> t p", p=P))

        x_raw = {}
        w_raw = {}

        def load_x_half(half):
            for a in range(half * TILES_PER_HALF, (half + 1) * TILES_PER_HALF):
                raw = x_pool.tile([P, D], BF16, tag="x_raw", bufs=TOKEN_TILES)
                nc.sync.dma_start(out=raw[:], in_=x_rows[a * P : (a + 1) * P, :])
                x_raw[a] = raw

        def load_weight_chunk(c, w):
            for g in range(PASSES):
                raw = w_pool.tile([P, PACK, CHUNK], BF16, tag="w_raw")
                nc.sync.dma_start(
                    out=raw[:],
                    in_=weights[w][g * K_PASS : (g + 1) * K_PASS, c * CHUNK : (c + 1) * CHUNK].rearrange(
                        "(p j) c -> p j c", j=PACK
                    ),
                )
                w_raw[(c, w, g)] = raw

        load_x_half(0)
        load_weight_chunk(0, KEY)
        load_x_half(1)
        load_weight_chunk(0, VALUE)
        for c, w in product(range(1, CHUNKS), range(WEIGHTS)):
            load_weight_chunk(c, w)

        ident = consts.tile([P, P], F32)
        make_identity(nc, ident[:])

        warm = consts.tile([P, 1], F32)
        nc.vector.memset(warm[:], 0.0)
        nc.scalar.activation(out=warm[:], in_=warm[:], func=ACT.Exp)

        sums = consts.tile([P, P], F32)
        nc.vector.memset(sums[:], 0.0)

        x_grouped = {}
        x_quant = {}

        def transpose_x_half(half):
            grouped = x_pool.tile([P, PASSES * N_MOVE * PACK], BF16, align_bytes=64, tag="x_grouped", bufs=HALVES)
            grouped_words = grouped[:].bitcast(F32).rearrange("p (g t u) -> p g t u", g=PASSES, u=WORDS)
            for a in range(TILES_PER_HALF):
                words = (
                    x_raw[half * TILES_PER_HALF + a][:]
                    .bitcast(F32)
                    .rearrange("p (g q u) -> p g u q", g=PASSES, u=WORDS)
                )
                transposed = psum.tile([P, PASSES, WORDS, P], F32, tag=bank_tags[a % 2])
                for g, u in product(range(PASSES), range(WORDS)):
                    nc.tensor.transpose(out=transposed[:, g, u, :], in_=words[:, g, u, :], identity=ident[:])
                nc.scalar.copy(
                    out=grouped_words[:, :, a * P : (a + 1) * P, :],
                    in_=transposed[:].rearrange("p g u t -> p g t u"),
                )
            x_grouped[half] = grouped

        def quantise_x_half(half):
            for g in range(PASSES):
                codes = x_pool.tile([P, N_MOVE], U32, align_bytes=64, tag="x_codes", bufs=HALVES * PASSES)
                scales = x_pool.tile([P, N_MOVE], U8, align_bytes=64, tag="x_scales", bufs=HALVES * PASSES)
                nc.vector.quantize_mx(
                    out=codes[:].bitcast(FP8X4),
                    scales=scales[:],
                    in_=x_grouped[half][:, g * N_MOVE * PACK : (g + 1) * N_MOVE * PACK],
                )
                x_quant[(g, half)] = (codes, scales)

        w_grouped = {}
        w_quant = {}

        def regroup_weight_piece(c, w, g, engine):
            if c not in w_grouped:
                w_grouped[c] = group_pool.tile(
                    [P, WEIGHTS, PASSES, CHUNK, PACK], BF16, align_bytes=64, name="w_grouped", tag="w_grouped"
                )
            grouped = w_grouped[c][:, w, g]
            raw = w_raw[(c, w, g)][:]
            if engine == "gpsimd":
                nc.gpsimd.tensor_scalar(
                    out=grouped,
                    in0=raw.rearrange("p j c -> p c j"),
                    scalar1=1.0,
                    scalar2=0.0,
                    op0=ALU.mult,
                    op1=ALU.add,
                )
            else:
                copy = nc.vector.tensor_copy if engine == "vector" else nc.scalar.copy
                copy(
                    out=grouped.rearrange("p (c i) j -> p c j i", i=RUN),
                    in_=raw.rearrange("p j (c i) -> p c j i", i=RUN),
                )

        def quantise_weight_chunk(c, w):
            codes = w_pool.tile([P, PASSES, CHUNK], U32, align_bytes=64, tag="w_codes", bufs=WEIGHTS * CHUNKS)
            scales = w_pool.tile([P, PASSES, CHUNK], U8, align_bytes=64, tag="w_scales", bufs=WEIGHTS * CHUNKS)
            nc.vector.quantize_mx(
                out=codes[:].rearrange("p g c -> p (g c)").bitcast(FP8X4),
                scales=scales[:].rearrange("p g c -> p (g c)"),
                in_=w_grouped[c][:, w].rearrange("p g c j -> p (g c j)"),
            )
            w_quant[(c, w)] = (codes, scales)

        def unit_place(i):
            c, rest = divmod(i, UNITS_PER_CHUNK)
            half, local = divmod(rest, TILES_PER_CHUNK)
            return c, local, half

        def multiply(w, i, acc):
            c, local, half = unit_place(i)
            cols = slice(local * P, (local + 1) * P)
            w_codes, w_scales = w_quant[(c, w)]
            for g in range(PASSES):
                x_codes, x_scales = x_quant[(g, half)]
                nc.tensor.matmul_mx(
                    out=acc[:],
                    lhsT=w_codes[:, g, cols].bitcast(FP8X4),
                    lhsT_scale=w_scales[:, g, cols],
                    rhs=x_codes[:].bitcast(FP8X4),
                    rhs_scale=x_scales[:],
                    start=(g == 0),
                    stop=(g == PASSES - 1),
                )

        key_acc = {}
        value_acc = {}
        relu_minus_v = {}
        exp_min_v_0 = {}

        def stage_keys(i):
            c, local, half = unit_place(i)
            t = c * TILES_PER_CHUNK + local
            key_acc[i] = psum.tile([P, N_MOVE], F32, tag="key_acc", name="key_acc")
            multiply(KEY, i, key_acc[i])
            relu_minus_v[i] = work.tile([P, N_MOVE], F32, tag="relu_minus_v", name="relu_minus_v")
            nc.scalar.activation(
                out=relu_minus_v[i][:], in_=key_acc[i][:], func=ACT.Relu, scale=-1.0, bias=minus_bk[:, t : t + 1]
            )

        def stage_exp(i):
            exp_min_v_0[i] = work.tile([P, N_MOVE], F32, tag="exp_min_v_0", name="exp_min_v_0")
            nc.scalar.activation(out=exp_min_v_0[i][:], in_=relu_minus_v[i][:], func=ACT.Exp, scale=-1.0)

        def stage_values(i):
            value_acc[i] = psum.tile([P, N_MOVE], F32, tag="value_acc", name="value_acc")
            multiply(VALUE, i, value_acc[i])

        def stage_sums(i):
            c, local, half = unit_place(i)
            t = c * TILES_PER_CHUNK + local
            k_feat = work.tile([P, N_MOVE], F32, tag="k_feat")
            k_value = work.tile([P, N_MOVE], F32, tag="k_value")
            for b in range(BATCHES_PER_HALF):
                toks = slice(b * SEQ, (b + 1) * SEQ)
                ksum_col = BATCHES * H_TILES + (half * BATCHES_PER_HALF + b) * H_TILES + t
                nc.vector.scalar_tensor_tensor(
                    out=k_feat[:, toks],
                    in0=key_acc[i][:, toks],
                    scalar=bk_plus_1[:, t : t + 1],
                    in1=exp_min_v_0[i][:, toks],
                    op0=ALU.add,
                    op1=ALU.max,
                    accum_out=sums[:, ksum_col : ksum_col + 1],
                )
            for b in range(BATCHES_PER_HALF):
                toks = slice(b * SEQ, (b + 1) * SEQ)
                kv_col = (half * BATCHES_PER_HALF + b) * H_TILES + t
                nc.vector.scalar_tensor_tensor(
                    out=k_value[:, toks],
                    in0=value_acc[i][:, toks],
                    scalar=bv_cols[:, t : t + 1],
                    in1=k_feat[:, toks],
                    op0=ALU.add,
                    op1=ALU.mult,
                    accum_out=sums[:, kv_col : kv_col + 1],
                )

        transpose_x_half(0)

        bias_rows_f32 = consts.tile([P, P], F32)
        nc.vector.tensor_copy(out=bias_rows_f32[:], in_=bias_rows[:])
        bias_ps = psum.tile([P, P], F32, tag="key_acc")
        nc.tensor.transpose(out=bias_ps[:], in_=bias_rows_f32[:], identity=ident[:])
        bv_cols = consts.tile([P, H_TILES], F32)
        nc.vector.tensor_copy(out=bv_cols[:], in_=bias_ps[:, H_TILES : 2 * H_TILES])
        bk_plus_1 = consts.tile([P, H_TILES], F32)
        nc.vector.tensor_scalar_add(out=bk_plus_1[:], in0=bias_ps[:, 0:H_TILES], scalar1=1.0)
        minus_bk = consts.tile([P, H_TILES], F32)
        nc.vector.tensor_scalar_mul(out=minus_bk[:], in0=bias_ps[:, 0:H_TILES], scalar1=-1.0)

        for g in range(PASSES):
            regroup_weight_piece(0, KEY, g, "vector")
        quantise_x_half(0)
        quantise_weight_chunk(0, KEY)
        transpose_x_half(1)
        for g in range(PASSES):
            regroup_weight_piece(0, VALUE, g, "vector")
        quantise_weight_chunk(0, VALUE)
        quantise_x_half(1)

        pieces = list(product(range(WEIGHTS), range(PASSES)))
        for w, g in pieces[:GPSIMD_PIECES]:
            regroup_weight_piece(1, w, g, "gpsimd")

        for i in range(-KEYS_AHEAD, UNITS):
            if 0 <= i + EXP_AHEAD < UNITS:
                stage_exp(i + EXP_AHEAD)
            if i + KEYS_AHEAD < UNITS:
                stage_keys(i + KEYS_AHEAD)
            if 0 <= i + EXP_AHEAD < UNITS:
                stage_values(i + EXP_AHEAD)
            if i < 0:
                continue
            c, place_in_chunk = divmod(i, UNITS_PER_CHUNK)
            more_chunks = c + 1 < CHUNKS
            if more_chunks and place_in_chunk < len(pieces) - GPSIMD_PIECES:
                regroup_weight_piece(c + 1, *pieces[GPSIMD_PIECES + place_in_chunk], "scalar")
            stage_sums(i)
            if more_chunks and place_in_chunk == UNITS_PER_CHUNK - KEYS_AHEAD - 1:
                quantise_weight_chunk(c + 1, KEY)
            if more_chunks and place_in_chunk == UNITS_PER_CHUNK - EXP_AHEAD - 1:
                quantise_weight_chunk(c + 1, VALUE)
                if c + 2 < CHUNKS:
                    for w, g in pieces[:GPSIMD_PIECES]:
                        regroup_weight_piece(c + 2, w, g, "gpsimd")

        sums_ps = psum.tile([P, P], F32, tag="key_acc")
        nc.tensor.transpose(out=sums_ps[:], in_=sums[:], identity=ident[:])
        result = consts.tile([P, P], F32)
        nc.vector.tensor_copy(out=result[:], in_=sums_ps[:])
        rows = BATCHES * H_TILES
        nc.sync.dma_start(out=out_0.rearrange("n (t p) -> (n t) p", p=P), in_=result[0:rows, :])
        nc.sync.dma_start(out=out_1.rearrange("n (t p) -> (n t) p", p=P), in_=result[rows : 2 * rows, :])
